import numpy as np
import ml_dtypes


def mxq(x, axis, fmt="e4m3"):
    dtype, down = {"e4m3": (ml_dtypes.float8_e4m3fn, 7), "e5m2": (ml_dtypes.float8_e5m2, 14)}[fmt]
    v = np.moveaxis(np.asarray(x, np.float32).astype(ml_dtypes.bfloat16).astype(np.float64), axis, -1)
    blocks = v.reshape(v.shape[:-1] + (-1, 32))
    amax = np.abs(blocks).max(-1, keepdims=True)
    byte = np.maximum(np.where(amax > 0, np.frexp(amax)[1] - 1 + 127, 0) - down, 1)
    scale = np.exp2(byte - 127.0)
    codes = (blocks / scale).astype(np.float32).astype(dtype).astype(np.float64)
    return np.moveaxis((codes * scale).reshape(v.shape), -1, axis)


WIDE = False


def mx_kscale(k):
    if not WIDE:
        return np.ones(k)
    levels = np.array([10, -10, 5, -5, 0])
    a = np.random.permutation(np.resize(levels, k // 512 * 4)).reshape(k // 512, 4)
    idx = np.arange(k)
    return np.exp2(a[idx // 512, idx % 128 // 32])


BF16 = ml_dtypes.bfloat16


def bf(x):
    return np.asarray(x, np.float32).astype(BF16)


def f64(x):
    return np.asarray(x).astype(np.float64)


B, S, H, F = 512, 8, 512, 512


def setup_inputs():
    s = mx_kscale(H)
    t = mx_kscale(F)
    s2 = np.concatenate([s, s])
    return {"h": bf(np.random.standard_normal((B, S, H)) * s),
            "ew1": bf(np.random.standard_normal((2 * H, F)) / np.sqrt(2 * H) / s2[:, None] * t),
            "eb1": bf(np.random.standard_normal(F) * 0.3 * t),
            "ew2": bf(np.random.standard_normal((F, H)) / np.sqrt(F) / t[:, None]),
            "eb2": bf(np.random.standard_normal(H) * 0.3)}


def edge_mlp(xq, w1q, b1, w2q, b2):
    hid = np.maximum((xq @ w1q) + b1, 0.0)
    return (mxq(hid, 2, "e4m3") @ w2q) + b2


def reference(h, ew1, eb1, ew2, eb2):
    hq = mxq(f64(h), 2, "e4m3")
    w1q = mxq(f64(ew1), 0, "e4m3")
    w2q = mxq(f64(ew2), 0, "e4m3")
    b1, b2 = f64(eb1), f64(eb2)
    left = hq[:, :-1, :]
    right = hq[:, 1:, :]
    m_lr = edge_mlp(np.concatenate([left, right], axis=-1), w1q, b1, w2q, b2)
    m_rl = edge_mlp(np.concatenate([right, left], axis=-1), w1q, b1, w2q, b2)
    zcol = np.zeros_like(m_lr[:, :1, :])
    return np.concatenate([zcol, m_lr], axis=1) + np.concatenate([m_rl, zcol], axis=1)

@@ -1,0 +1,228 @@
+from contextlib import ExitStack
+
+import concourse.mybir as mybir
+from concourse.masks import make_identity
+
+BF16 = mybir.dt.bfloat16
+F32 = mybir.dt.float32
+U32 = mybir.dt.uint32
+U8 = mybir.dt.uint8
+FP8X4 = mybir.dt.float8_e4m3fn_x4
+RELU = mybir.ActivationFunctionType.Relu
+COPY = mybir.ActivationFunctionType.Copy
+ADD = mybir.AluOpType.add
+
+P = 128
+PACK = 4
+CHAINS, NODES, WIDTH = 512, 8, 512
+EDGES = NODES - 1
+CHAIN_TILES = CHAINS // P
+CHUNKS = WIDTH // P
+WORDS = WIDTH // 2
+LR, RL = "lr", "rl"
+
+FLOPS = 2 * 2 * CHAINS * EDGES * (2 * WIDTH * WIDTH + WIDTH * WIDTH)
+
+
+def tile_graphnetlayer_pa_t_kernel(tc, h, ew1, eb1, ew2, eb2, out):
+    nc = tc.nc
+    with ExitStack() as stack:
+        stack.enter_context(tc.manual_schedule())
+        consts = stack.enter_context(tc.tile_pool(name="consts", bufs=1))
+        weights = stack.enter_context(tc.tile_pool(name="weights", bufs=1))
+        nodes = stack.enter_context(tc.tile_pool(name="nodes", bufs=1))
+        h_raw_pool = stack.enter_context(tc.tile_pool(name="h_raw_pool", bufs=NODES))
+        h_grouped_pool = stack.enter_context(tc.tile_pool(name="h_grouped_pool", bufs=2))
+        planes_pool = stack.enter_context(tc.tile_pool(name="planes_pool", bufs=2))
+        hid_grouped_pool = stack.enter_context(tc.tile_pool(name="hid_grouped_pool", bufs=2))
+        hid_pool = stack.enter_context(tc.tile_pool(name="hid_pool", bufs=6))
+        result_pool = stack.enter_context(tc.tile_pool(name="result_pool", bufs=6))
+        acc1_pool = stack.enter_context(tc.psum_pool(name="acc1_pool", bufs=4))
+        aux_pool = stack.enter_context(tc.psum_pool(name="aux_pool", bufs=4))
+
+        w1_raw = weights.tile([P, 2, PACK, WIDTH], BF16)
+        for a in range(2):
+            nc.sync.dma_start(
+                out=w1_raw[:, a, :, :].rearrange("q (u e) f -> q u e f", u=2),
+                in_=ew1[a * WIDTH : (a + 1) * WIDTH, :].rearrange("(u q e) f -> q u e f", u=2, e=2),
+            )
+
+        def load_node(s):
+            raw = h_raw_pool.tile([P, CHAIN_TILES * WIDTH], BF16, name="h_raw", tag="h_raw")
+            nc.sync.dma_start(
+                out=raw[:].rearrange("p (t k) -> p t k", t=CHAIN_TILES),
+                in_=h[:, s, :].rearrange("(t p) k -> p t k", p=P),
+            )
+            return raw
+
+        h_raw = [load_node(s) for s in range(2)]
+        w2_raw = weights.tile([P, PACK, WIDTH], BF16)
+        nc.sync.dma_start(out=w2_raw[:], in_=ew2.rearrange("(p t) n -> p t n", t=PACK))
+        h_raw.extend([load_node(s) for s in range(2, NODES)])
+
+        ones = consts.tile([P, P], BF16)
+        nc.vector.memset(ones[:], 1.0)
+        b2_rows = consts.tile([P, WIDTH], BF16)
+        nc.vector.memset(b2_rows[:], 0.0)
+        nc.scalar.dma_start(out=b2_rows[0:1, :], in_=eb2.rearrange("(o n) -> o n", o=1))
+
+        b1_bf16 = consts.tile([P, CHUNKS], BF16)
+        nc.scalar.dma_start(out=b1_bf16[:], in_=eb1.rearrange("(p c) -> p c", c=CHUNKS))
+        b1 = consts.tile([P, CHUNKS], F32)
+        nc.vector.tensor_copy(out=b1[:], in_=b1_bf16[:])
+
+        b2_spread = aux_pool.tile([P, WIDTH], F32, tag="aux")
+        nc.tensor.matmul(out=b2_spread[:], lhsT=ones[:], rhs=b2_rows[:], start=True, stop=True)
+        b2_once = consts.tile([P, WIDTH], F32)
+        nc.scalar.copy(out=b2_once[:], in_=b2_spread[:])
+        b2_twice = consts.tile([P, WIDTH], F32)
+        nc.scalar.activation(out=b2_twice[:], in_=b2_spread[:], func=COPY, scale=2.0)
+
+        ident = consts.tile([P, P], F32)
+        make_identity(nc, ident[:])
+
+        w1_grouped = weights.tile([P, 2, CHUNKS, P, PACK], BF16, align_bytes=64)
+        w1_codes = weights.tile([P, 2, WIDTH], U32, align_bytes=64)
+        w1_scales = weights.tile([P, 2, WIDTH], U8, align_bytes=64)
+        for a in range(2):
+            nc.vector.tensor_copy(
+                out=w1_grouped[:, a, :, :, :],
+                in_=w1_raw[:, a, :, :].rearrange("q t (m c) -> q c m t", c=CHUNKS),
+            )
+        for a in range(2):
+            nc.vector.quantize_mx(
+                out=w1_codes[:, a, :].bitcast(FP8X4),
+                scales=w1_scales[:, a, :],
+                in_=w1_grouped[:, a, :, :, :].rearrange("q c m t -> q (c m t)"),
+            )
+
+        w2_grouped = weights.tile([P, WIDTH, PACK], BF16, align_bytes=64)
+        w2_codes = weights.tile([P, WIDTH], U32, align_bytes=64)
+        w2_scales = weights.tile([P, WIDTH], U8, align_bytes=64)
+
+        def regroup(grouped, planes):
+            nc.vector.tensor_copy(
+                out=grouped[:].rearrange("p (c i) t -> p c t i", i=4),
+                in_=planes[:].rearrange("p t (c i) -> p c t i", i=4),
+            )
+
+        h_codes = nodes.tile([P, NODES, CHAINS], U32, align_bytes=64)
+        h_scales = nodes.tile([P, NODES, CHAINS], U8, align_bytes=64)
+        h_grouped = {}
+
+        def transpose_node(s):
+            words = h_raw[s][:].bitcast(F32)
+            grouped = h_grouped_pool.tile([P, CHAINS * PACK], BF16, name="h_grouped", tag="h_grouped", align_bytes=64)
+            grouped_words = grouped[:].bitcast(F32).rearrange("p (c u) -> p c u", u=2)
+            for half in range(2):
+                bank = aux_pool.tile([P, 2, 2 * P], F32, tag="aux")
+                for u in range(2):
+                    for l in range(2):
+                        first = (2 * half + l) * WORDS + u * P
+                        nc.tensor.transpose(bank[:, u, l * P : (l + 1) * P], words[:, first : first + P], ident[:])
+                nc.scalar.copy(
+                    out=grouped_words[:, half * 2 * P : (half + 1) * 2 * P, :],
+                    in_=bank[:].rearrange("p u c -> p c u"),
+                )
+            h_grouped[s] = grouped
+
+        def quantise_node(s):
+            nc.vector.quantize_mx(
+                out=h_codes[:, s, :].bitcast(FP8X4), scales=h_scales[:, s, :], in_=h_grouped[s][:]
+            )
+
+        planes = {}
+        hid_grouped = {}
+        hid_codes = {}
+        hid_scales = {}
+
+        def layer1(i, direction):
+            joined = (i, i + 1) if direction == LR else (i + 1, i)
+            hidden = planes_pool.tile([P, CHUNKS, CHAINS], BF16, name="planes", tag="planes")
+            for c in range(CHUNKS):
+                acc1 = acc1_pool.tile([P, CHAINS], F32)
+                for a in range(2):
+                    nc.tensor.matmul_mx(
+                        out=acc1[:],
+                        lhsT=w1_codes[:, a, c * P : (c + 1) * P].bitcast(FP8X4),
+                        lhsT_scale=w1_scales[:, a, c * P : (c + 1) * P],
+                        rhs=h_codes[:, joined[a], :].bitcast(FP8X4),
+                        rhs_scale=h_scales[:, joined[a], :],
+                        start=(a == 0),
+                        stop=(a == 1),
+                    )
+                nc.scalar.activation(out=hidden[:, c, :], in_=acc1[:], func=RELU, bias=b1[:, c : c + 1], scale=1.0)
+            planes[(i, direction)] = hidden
+
+        def regroup_hidden(i, direction):
+            grouped = hid_grouped_pool.tile([P, CHAINS, PACK], BF16, name="hid_grouped", tag="hid_grouped", align_bytes=64)
+            regroup(grouped, planes[(i, direction)])
+            hid_grouped[(i, direction)] = grouped
+
+        def quantise_hidden(i, direction):
+            codes = hid_pool.tile([P, CHAINS], U32, name="hid_codes", tag="hid_codes", align_bytes=64)
+            scales = hid_pool.tile([P, CHAINS], U8, name="hid_scales", tag="hid_scales", align_bytes=64)
+            nc.vector.quantize_mx(
+                out=codes[:].bitcast(FP8X4),
+                scales=scales[:],
+                in_=hid_grouped[(i, direction)][:].rearrange("p w t -> p (w t)"),
+            )
+            hid_codes[(i, direction)] = codes
+            hid_scales[(i, direction)] = scales
+
+        def layer2(j, chain_tiles):
+            messages = []
+            if j > 0:
+                messages.append((j - 1, LR))
+            if j < EDGES:
+                messages.append((j, RL))
+            bias = b2_twice if len(messages) == 2 else b2_once
+            for t in chain_tiles:
+                acc2 = aux_pool.tile([P, WIDTH], F32, tag="aux")
+                for n, message in enumerate(messages):
+                    nc.tensor.matmul_mx(
+                        out=acc2[:],
+                        lhsT=hid_codes[message][:, t * P : (t + 1) * P].bitcast(FP8X4),
+                        lhsT_scale=hid_scales[message][:, t * P : (t + 1) * P],
+                        rhs=w2_codes[:].bitcast(FP8X4),
+                        rhs_scale=w2_scales[:],
+                        start=(n == 0),
+                        stop=(n == len(messages) - 1),
+                    )
+                result = result_pool.tile([P, WIDTH], F32)
+                nc.vector.tensor_tensor(out=result[:], in0=acc2[:], in1=bias[:], op=ADD)
+                nc.sync.dma_start(out=out[t * P : (t + 1) * P, j, :], in_=result[:])
+
+        first_tiles = range(CHAIN_TILES // 2)
+        last_tiles = range(CHAIN_TILES // 2, CHAIN_TILES)
+
+        for s in range(2):
+            transpose_node(s)
+            quantise_node(s)
+
+        for i in range(EDGES):
+            layer1(i, RL)
+            if i + 2 < NODES:
+                transpose_node(i + 2)
+            regroup_hidden(i, RL)
+            if i == 0:
+                regroup(w2_grouped, w2_raw)
+            else:
+                layer2(i - 1, first_tiles)
+            if i + 2 < NODES:
+                quantise_node(i + 2)
+            quantise_hidden(i, RL)
+            layer1(i, LR)
+            regroup_hidden(i, LR)
+            if i == 0:
+                nc.vector.quantize_mx(
+                    out=w2_codes[:].bitcast(FP8X4),
+                    scales=w2_scales[:],
+                    in_=w2_grouped[:].rearrange("p w t -> p (w t)"),
+                )
+            else:
+                layer2(i - 1, last_tiles)
+            quantise_hidden(i, LR)
+
+        layer2(EDGES - 1, range(CHAIN_TILES))
+        layer2(EDGES, range(CHAIN_TILES))

@@ -9,17 +9,20 @@ U32 = mybir.dt.uint32
 U8 = mybir.dt.uint8
 FP8X4 = mybir.dt.float8_e4m3fn_x4
 RELU = mybir.ActivationFunctionType.Relu
-COPY = mybir.ActivationFunctionType.Copy
+IDENTITY = mybir.ActivationFunctionType.Identity
 ADD = mybir.AluOpType.add
+MULT = mybir.AluOpType.mult
 
 P = 128
 PACK = 4
 CHAINS, NODES, WIDTH = 512, 8, 512
 EDGES = NODES - 1
-CHAIN_TILES = CHAINS // P
 CHUNKS = WIDTH // P
 WORDS = WIDTH // 2
-LR, RL = "lr", "rl"
+HALVES = 2
+HALF = CHAINS // HALVES
+HALF_TILES = HALF // P
+LR, RL = 0, 1
 
 FLOPS = 2 * 2 * CHAINS * EDGES * (2 * WIDTH * WIDTH + WIDTH * WIDTH)
 
@@ -31,14 +34,32 @@ def tile_graphnetlayer_pa_t_kernel(tc, h, ew1, eb1, ew2, eb2, out):
         consts = stack.enter_context(tc.tile_pool(name="consts", bufs=1))
         weights = stack.enter_context(tc.tile_pool(name="weights", bufs=1))
         nodes = stack.enter_context(tc.tile_pool(name="nodes", bufs=1))
-        h_raw_pool = stack.enter_context(tc.tile_pool(name="h_raw_pool", bufs=NODES))
-        h_grouped_pool = stack.enter_context(tc.tile_pool(name="h_grouped_pool", bufs=2))
+        h_raw_pool = stack.enter_context(tc.tile_pool(name="h_raw_pool", bufs=HALVES * NODES // 2))
+        h_grouped_pool = stack.enter_context(tc.tile_pool(name="h_grouped_pool", bufs=4))
         planes_pool = stack.enter_context(tc.tile_pool(name="planes_pool", bufs=2))
         hid_grouped_pool = stack.enter_context(tc.tile_pool(name="hid_grouped_pool", bufs=2))
         hid_pool = stack.enter_context(tc.tile_pool(name="hid_pool", bufs=6))
         result_pool = stack.enter_context(tc.tile_pool(name="result_pool", bufs=6))
         acc1_pool = stack.enter_context(tc.psum_pool(name="acc1_pool", bufs=4))
         aux_pool = stack.enter_context(tc.psum_pool(name="aux_pool", bufs=4))
+
+        b1_bf16 = consts.tile([P, CHUNKS], BF16)
+        nc.scalar.dma_start(out=b1_bf16[:], in_=eb1.rearrange("(p c) -> p c", c=CHUNKS))
+        b1 = consts.tile([P, CHUNKS], F32)
+        ones = consts.tile([P, P], BF16)
+        nc.vector.memset(ones[:], 1.0)
+        b2_rows = consts.tile([P, WIDTH], BF16)
+        nc.vector.memset(b2_rows[:], 0.0)
+        nc.scalar.dma_start(out=b2_rows[0:1, :], in_=eb2.rearrange("(o n) -> o n", o=1))
+        nc.scalar.activation(out=b1[:], in_=b1_bf16[:], func=IDENTITY)
+        b2_once = consts.tile([P, WIDTH], F32)
+        b2_twice = consts.tile([P, WIDTH], F32)
+
+        def spread_b2():
+            b2_spread = aux_pool.tile([P, WIDTH], F32, tag="aux")
+            nc.tensor.matmul(out=b2_spread[:], lhsT=ones[:], rhs=b2_rows[:], start=True, stop=True)
+            nc.vector.tensor_copy(out=b2_once[:], in_=b2_spread[:])
+            nc.vector.tensor_scalar(out=b2_twice[:], in0=b2_spread[:], scalar1=2.0, scalar2=None, op0=MULT)
 
         w1_raw = weights.tile([P, 2, PACK, WIDTH], BF16)
         for a in range(2):
@@ -47,36 +68,22 @@ def tile_graphnetlayer_pa_t_kernel(tc, h, ew1, eb1, ew2, eb2, out):
                 in_=ew1[a * WIDTH : (a + 1) * WIDTH, :].rearrange("(u q e) f -> q u e f", u=2, e=2),
             )
 
-        def load_node(s):
-            raw = h_raw_pool.tile([P, CHAIN_TILES * WIDTH], BF16, name="h_raw", tag="h_raw")
-            nc.sync.dma_start(
-                out=raw[:].rearrange("p (t k) -> p t k", t=CHAIN_TILES),
-                in_=h[:, s, :].rearrange("(t p) k -> p t k", p=P),
-            )
-            return raw
+        h_raw = {}
 
-        h_raw = [load_node(s) for s in range(2)]
+        def load_node_pair(g):
+            for half in range(HALVES):
+                raw = h_raw_pool.tile([P, HALF_TILES * 2 * WIDTH], BF16, name="h_raw", tag="h_raw")
+                nc.sync.dma_start(
+                    out=raw[:].rearrange("p (t s k) -> p t s k", t=HALF_TILES, s=2),
+                    in_=h[half * HALF : (half + 1) * HALF, 2 * g : 2 * g + 2, :].rearrange("(t p) s k -> p t s k", p=P),
+                )
+                h_raw[(g, half)] = raw
+
+        load_node_pair(0)
         w2_raw = weights.tile([P, PACK, WIDTH], BF16)
         nc.sync.dma_start(out=w2_raw[:], in_=ew2.rearrange("(p t) n -> p t n", t=PACK))
-        h_raw.extend([load_node(s) for s in range(2, NODES)])
-
-        ones = consts.tile([P, P], BF16)
-        nc.vector.memset(ones[:], 1.0)
-        b2_rows = consts.tile([P, WIDTH], BF16)
-        nc.vector.memset(b2_rows[:], 0.0)
-        nc.scalar.dma_start(out=b2_rows[0:1, :], in_=eb2.rearrange("(o n) -> o n", o=1))
-
-        b1_bf16 = consts.tile([P, CHUNKS], BF16)
-        nc.scalar.dma_start(out=b1_bf16[:], in_=eb1.rearrange("(p c) -> p c", c=CHUNKS))
-        b1 = consts.tile([P, CHUNKS], F32)
-        nc.vector.tensor_copy(out=b1[:], in_=b1_bf16[:])
-
-        b2_spread = aux_pool.tile([P, WIDTH], F32, tag="aux")
-        nc.tensor.matmul(out=b2_spread[:], lhsT=ones[:], rhs=b2_rows[:], start=True, stop=True)
-        b2_once = consts.tile([P, WIDTH], F32)
-        nc.scalar.copy(out=b2_once[:], in_=b2_spread[:])
-        b2_twice = consts.tile([P, WIDTH], F32)
-        nc.scalar.activation(out=b2_twice[:], in_=b2_spread[:], func=COPY, scale=2.0)
+        for g in range(1, NODES // 2):
+            load_node_pair(g)
 
         ident = consts.tile([P, P], F32)
         make_identity(nc, ident[:])
@@ -110,25 +117,24 @@ def tile_graphnetlayer_pa_t_kernel(tc, h, ew1, eb1, ew2, eb2, out):
         h_scales = nodes.tile([P, NODES, CHAINS], U8, align_bytes=64)
         h_grouped = {}
 
-        def transpose_node(s):
-            words = h_raw[s][:].bitcast(F32)
-            grouped = h_grouped_pool.tile([P, CHAINS * PACK], BF16, name="h_grouped", tag="h_grouped", align_bytes=64)
-            grouped_words = grouped[:].bitcast(F32).rearrange("p (c u) -> p c u", u=2)
-            for half in range(2):
-                bank = aux_pool.tile([P, 2, 2 * P], F32, tag="aux")
-                for u in range(2):
-                    for l in range(2):
-                        first = (2 * half + l) * WORDS + u * P
-                        nc.tensor.transpose(bank[:, u, l * P : (l + 1) * P], words[:, first : first + P], ident[:])
-                nc.scalar.copy(
-                    out=grouped_words[:, half * 2 * P : (half + 1) * 2 * P, :],
-                    in_=bank[:].rearrange("p u c -> p c u"),
-                )
-            h_grouped[s] = grouped
+        def transpose_node(s, half):
+            words = h_raw[(s // 2, half)][:].bitcast(F32)
+            bank = aux_pool.tile([P, 2, HALF], F32, tag="aux")
+            for u in range(2):
+                for t in range(HALF_TILES):
+                    first = (2 * t + s % 2) * WORDS + u * P
+                    nc.tensor.transpose(bank[:, u, t * P : (t + 1) * P], words[:, first : first + P], ident[:])
+            grouped = h_grouped_pool.tile([P, HALF * PACK], BF16, name="h_grouped", tag="h_grouped", align_bytes=64)
+            nc.scalar.copy(
+                out=grouped[:].bitcast(F32).rearrange("p (c u) -> p c u", u=2),
+                in_=bank[:].rearrange("p u c -> p c u"),
+            )
+            h_grouped[(s, half)] = grouped
 
-        def quantise_node(s):
+        def quantise_node(s, half):
+            chains = slice(half * HALF, (half + 1) * HALF)
             nc.vector.quantize_mx(
-                out=h_codes[:, s, :].bitcast(FP8X4), scales=h_scales[:, s, :], in_=h_grouped[s][:]
+                out=h_codes[:, s, chains].bitcast(FP8X4), scales=h_scales[:, s, chains], in_=h_grouped[(s, half)][:]
             )
 
         planes = {}
@@ -136,54 +142,58 @@ def tile_graphnetlayer_pa_t_kernel(tc, h, ew1, eb1, ew2, eb2, out):
         hid_codes = {}
         hid_scales = {}
 
-        def layer1(i, direction):
-            joined = (i, i + 1) if direction == LR else (i + 1, i)
-            hidden = planes_pool.tile([P, CHUNKS, CHAINS], BF16, name="planes", tag="planes")
+        def layer1(i, half):
+            chains = slice(half * HALF, (half + 1) * HALF)
+            hidden = planes_pool.tile([P, CHUNKS, 2, HALF], BF16, name="planes", tag="planes")
             for c in range(CHUNKS):
-                acc1 = acc1_pool.tile([P, CHAINS], F32)
-                for a in range(2):
-                    nc.tensor.matmul_mx(
-                        out=acc1[:],
-                        lhsT=w1_codes[:, a, c * P : (c + 1) * P].bitcast(FP8X4),
-                        lhsT_scale=w1_scales[:, a, c * P : (c + 1) * P],
-                        rhs=h_codes[:, joined[a], :].bitcast(FP8X4),
-                        rhs_scale=h_scales[:, joined[a], :],
-                        start=(a == 0),
-                        stop=(a == 1),
-                    )
-                nc.scalar.activation(out=hidden[:, c, :], in_=acc1[:], func=RELU, bias=b1[:, c : c + 1], scale=1.0)
-            planes[(i, direction)] = hidden
+                acc1 = acc1_pool.tile([P, 2, HALF], F32)
+                for direction, joined in ((LR, (i, i + 1)), (RL, (i + 1, i))):
+                    for a in range(2):
+                        nc.tensor.matmul_mx(
+                            out=acc1[:, direction, :],
+                            lhsT=w1_codes[:, a, c * P : (c + 1) * P].bitcast(FP8X4),
+                            lhsT_scale=w1_scales[:, a, c * P : (c + 1) * P],
+                            rhs=h_codes[:, joined[a], chains].bitcast(FP8X4),
+                            rhs_scale=h_scales[:, joined[a], chains],
+                            start=(a == 0),
+                            stop=(a == 1),
+                        )
+                nc.scalar.activation(
+                    out=hidden[:, c, :, :], in_=acc1[:], func=RELU, bias=b1[:, c : c + 1], scale=1.0
+                )
+            planes[(i, half)] = hidden
 
-        def regroup_hidden(i, direction):
-            grouped = hid_grouped_pool.tile([P, CHAINS, PACK], BF16, name="hid_grouped", tag="hid_grouped", align_bytes=64)
-            regroup(grouped, planes[(i, direction)])
-            hid_grouped[(i, direction)] = grouped
+        def regroup_hidden(i, half):
+            grouped = hid_grouped_pool.tile([P, 2 * HALF, PACK], BF16, name="hid_grouped", tag="hid_grouped", align_bytes=64)
+            regroup(grouped, planes[(i, half)][:].rearrange("p t d w -> p t (d w)"))
+            hid_grouped[(i, half)] = grouped
 
-        def quantise_hidden(i, direction):
-            codes = hid_pool.tile([P, CHAINS], U32, name="hid_codes", tag="hid_codes", align_bytes=64)
-            scales = hid_pool.tile([P, CHAINS], U8, name="hid_scales", tag="hid_scales", align_bytes=64)
+        def quantise_hidden(i, half):
+            codes = hid_pool.tile([P, 2 * HALF], U32, name="hid_codes", tag="hid_codes", align_bytes=64)
+            scales = hid_pool.tile([P, 2 * HALF], U8, name="hid_scales", tag="hid_scales", align_bytes=64)
             nc.vector.quantize_mx(
                 out=codes[:].bitcast(FP8X4),
                 scales=scales[:],
-                in_=hid_grouped[(i, direction)][:].rearrange("p w t -> p (w t)"),
+                in_=hid_grouped[(i, half)][:].rearrange("p w t -> p (w t)"),
             )
-            hid_codes[(i, direction)] = codes
-            hid_scales[(i, direction)] = scales
+            hid_codes[(i, half)] = codes
+            hid_scales[(i, half)] = scales
 
-        def layer2(j, chain_tiles):
+        def layer2(j, half):
             messages = []
             if j > 0:
                 messages.append((j - 1, LR))
             if j < EDGES:
                 messages.append((j, RL))
             bias = b2_twice if len(messages) == 2 else b2_once
-            for t in chain_tiles:
+            for t in range(HALF_TILES):
                 acc2 = aux_pool.tile([P, WIDTH], F32, tag="aux")
-                for n, message in enumerate(messages):
+                for n, (i, direction) in enumerate(messages):
+                    columns = slice(direction * HALF + t * P, direction * HALF + (t + 1) * P)
                     nc.tensor.matmul_mx(
                         out=acc2[:],
-                        lhsT=hid_codes[message][:, t * P : (t + 1) * P].bitcast(FP8X4),
-                        lhsT_scale=hid_scales[message][:, t * P : (t + 1) * P],
+                        lhsT=hid_codes[(i, half)][:, columns].bitcast(FP8X4),
+                        lhsT_scale=hid_scales[(i, half)][:, columns],
                         rhs=w2_codes[:].bitcast(FP8X4),
                         rhs_scale=w2_scales[:],
                         start=(n == 0),
@@ -191,38 +201,41 @@ def tile_graphnetlayer_pa_t_kernel(tc, h, ew1, eb1, ew2, eb2, out):
                     )
                 result = result_pool.tile([P, WIDTH], F32)
                 nc.vector.tensor_tensor(out=result[:], in0=acc2[:], in1=bias[:], op=ADD)
-                nc.sync.dma_start(out=out[t * P : (t + 1) * P, j, :], in_=result[:])
+                first_chain = half * HALF + t * P
+                nc.sync.dma_start(out=out[first_chain : first_chain + P, j, :], in_=result[:])
 
-        first_tiles = range(CHAIN_TILES // 2)
-        last_tiles = range(CHAIN_TILES // 2, CHAIN_TILES)
+        for half in range(HALVES):
+            for s in range(2):
+                transpose_node(s, half)
+        for half in range(HALVES):
+            for s in range(2):
+                quantise_node(s, half)
+        regroup(w2_grouped, w2_raw)
 
-        for s in range(2):
-            transpose_node(s)
-            quantise_node(s)
-
+        ready = []
         for i in range(EDGES):
-            layer1(i, RL)
-            if i + 2 < NODES:
-                transpose_node(i + 2)
-            regroup_hidden(i, RL)
-            if i == 0:
-                regroup(w2_grouped, w2_raw)
-            else:
-                layer2(i - 1, first_tiles)
-            if i + 2 < NODES:
-                quantise_node(i + 2)
-            quantise_hidden(i, RL)
-            layer1(i, LR)
-            regroup_hidden(i, LR)
-            if i == 0:
-                nc.vector.quantize_mx(
-                    out=w2_codes[:].bitcast(FP8X4),
-                    scales=w2_scales[:],
-                    in_=w2_grouped[:].rearrange("p w t -> p (w t)"),
-                )
-            else:
-                layer2(i - 1, last_tiles)
-            quantise_hidden(i, LR)
-
-        layer2(EDGES - 1, range(CHAIN_TILES))
-        layer2(EDGES, range(CHAIN_TILES))
+            for half in range(HALVES):
+                layer1(i, half)
+                if (i, half) == (0, 0):
+                    spread_b2()
+                    nc.vector.quantize_mx(
+                        out=w2_codes[:].bitcast(FP8X4),
+                        scales=w2_scales[:],
+                        in_=w2_grouped[:].rearrange("p w t -> p (w t)"),
+                    )
+                new_node = half == 0 and i + 2 < NODES
+                if new_node:
+                    for other in range(HALVES):
+                        transpose_node(i + 2, other)
+                regroup_hidden(i, half)
+                if new_node:
+                    for other in range(HALVES):
+                        quantise_node(i + 2, other)
+                quantise_hidden(i, half)
+                for j, earlier_half in ready:
+                    layer2(j, earlier_half)
+                ready = [(i, half)]
+                if i == EDGES - 1:
+                    ready.append((NODES - 1, half))
+        for j, earlier_half in ready:
+            layer2(j, earlier_half)

@@ -23,6 +23,7 @@ HALVES = 2
 HALF = CHAINS // HALVES
 HALF_TILES = HALF // P
 LR, RL = 0, 1
+LAG = 2
 
 FLOPS = 2 * 2 * CHAINS * EDGES * (2 * WIDTH * WIDTH + WIDTH * WIDTH)
 
@@ -212,30 +213,32 @@ def tile_graphnetlayer_pa_t_kernel(tc, h, ew1, eb1, ew2, eb2, out):
                 quantise_node(s, half)
         regroup(w2_grouped, w2_raw)
 
-        ready = []
-        for i in range(EDGES):
-            for half in range(HALVES):
-                layer1(i, half)
-                if (i, half) == (0, 0):
-                    spread_b2()
-                    nc.vector.quantize_mx(
-                        out=w2_codes[:].bitcast(FP8X4),
-                        scales=w2_scales[:],
-                        in_=w2_grouped[:].rearrange("p w t -> p (w t)"),
-                    )
-                new_node = half == 0 and i + 2 < NODES
-                if new_node:
-                    for other in range(HALVES):
-                        transpose_node(i + 2, other)
-                regroup_hidden(i, half)
-                if new_node:
-                    for other in range(HALVES):
-                        quantise_node(i + 2, other)
-                quantise_hidden(i, half)
-                for j, earlier_half in ready:
-                    layer2(j, earlier_half)
-                ready = [(i, half)]
-                if i == EDGES - 1:
-                    ready.append((NODES - 1, half))
-        for j, earlier_half in ready:
-            layer2(j, earlier_half)
+        def second_layer_after(unit):
+            i, half = unit
+            layer2(i, half)
+            if i == EDGES - 1:
+                layer2(NODES - 1, half)
+
+        units = [(i, half) for i in range(EDGES) for half in range(HALVES)]
+        for u, (i, half) in enumerate(units):
+            layer1(i, half)
+            if u == 0:
+                spread_b2()
+                nc.vector.quantize_mx(
+                    out=w2_codes[:].bitcast(FP8X4),
+                    scales=w2_scales[:],
+                    in_=w2_grouped[:].rearrange("p w t -> p (w t)"),
+                )
+            if u >= LAG:
+                second_layer_after(units[u - LAG])
+            new_node = half == 0 and i + 2 < NODES
+            if new_node:
+                for other in range(HALVES):
+                    transpose_node(i + 2, other)
+            regroup_hidden(i, half)
+            if new_node:
+                for other in range(HALVES):
+                    quantise_node(i + 2, other)
+            quantise_hidden(i, half)
+        for unit in units[len(units) - LAG :]:
+            second_layer_after(unit)

from contextlib import ExitStack

import concourse.mybir as mybir
from concourse.masks import make_identity

BF16 = mybir.dt.bfloat16
F32 = mybir.dt.float32
U32 = mybir.dt.uint32
U8 = mybir.dt.uint8
FP8X4 = mybir.dt.float8_e4m3fn_x4
RELU = mybir.ActivationFunctionType.Relu
IDENTITY = mybir.ActivationFunctionType.Identity
ADD = mybir.AluOpType.add
MULT = mybir.AluOpType.mult

P = 128
PACK = 4
CHAINS, NODES, WIDTH = 512, 8, 512
EDGES = NODES - 1
CHUNKS = WIDTH // P
WORDS = WIDTH // 2
HALVES = 2
HALF = CHAINS // HALVES
HALF_TILES = HALF // P
LR, RL = 0, 1
LAG = 2

FLOPS = 2 * 2 * CHAINS * EDGES * (2 * WIDTH * WIDTH + WIDTH * WIDTH)


def tile_graphnetlayer_pa_t_kernel(tc, h, ew1, eb1, ew2, eb2, out):
    nc = tc.nc
    with ExitStack() as stack:
        stack.enter_context(tc.manual_schedule())
        consts = stack.enter_context(tc.tile_pool(name="consts", bufs=1))
        weights = stack.enter_context(tc.tile_pool(name="weights", bufs=1))
        nodes = stack.enter_context(tc.tile_pool(name="nodes", bufs=1))
        h_raw_pool = stack.enter_context(tc.tile_pool(name="h_raw_pool", bufs=HALVES * NODES // 2))
        h_grouped_pool = stack.enter_context(tc.tile_pool(name="h_grouped_pool", bufs=4))
        planes_pool = stack.enter_context(tc.tile_pool(name="planes_pool", bufs=2))
        hid_grouped_pool = stack.enter_context(tc.tile_pool(name="hid_grouped_pool", bufs=2))
        hid_pool = stack.enter_context(tc.tile_pool(name="hid_pool", bufs=6))
        result_pool = stack.enter_context(tc.tile_pool(name="result_pool", bufs=6))
        acc1_pool = stack.enter_context(tc.psum_pool(name="acc1_pool", bufs=4))
        aux_pool = stack.enter_context(tc.psum_pool(name="aux_pool", bufs=4))

        b1_bf16 = consts.tile([P, CHUNKS], BF16)
        nc.scalar.dma_start(out=b1_bf16[:], in_=eb1.rearrange("(p c) -> p c", c=CHUNKS))
        b1 = consts.tile([P, CHUNKS], F32)
        ones = consts.tile([P, P], BF16)
        nc.vector.memset(ones[:], 1.0)
        b2_rows = consts.tile([P, WIDTH], BF16)
        nc.vector.memset(b2_rows[:], 0.0)
        nc.scalar.dma_start(out=b2_rows[0:1, :], in_=eb2.rearrange("(o n) -> o n", o=1))
        nc.scalar.activation(out=b1[:], in_=b1_bf16[:], func=IDENTITY)
        b2_once = consts.tile([P, WIDTH], F32)
        b2_twice = consts.tile([P, WIDTH], F32)

        def spread_b2():
            b2_spread = aux_pool.tile([P, WIDTH], F32, tag="aux")
            nc.tensor.matmul(out=b2_spread[:], lhsT=ones[:], rhs=b2_rows[:], start=True, stop=True)
            nc.vector.tensor_copy(out=b2_once[:], in_=b2_spread[:])
            nc.vector.tensor_scalar(out=b2_twice[:], in0=b2_spread[:], scalar1=2.0, scalar2=None, op0=MULT)

        w1_raw = weights.tile([P, 2, PACK, WIDTH], BF16)
        for a in range(2):
            nc.sync.dma_start(
                out=w1_raw[:, a, :, :].rearrange("q (u e) f -> q u e f", u=2),
                in_=ew1[a * WIDTH : (a + 1) * WIDTH, :].rearrange("(u q e) f -> q u e f", u=2, e=2),
            )

        h_raw = {}

        def load_node_pair(g):
            for half in range(HALVES):
                raw = h_raw_pool.tile([P, HALF_TILES * 2 * WIDTH], BF16, name="h_raw", tag="h_raw")
                nc.sync.dma_start(
                    out=raw[:].rearrange("p (t s k) -> p t s k", t=HALF_TILES, s=2),
                    in_=h[half * HALF : (half + 1) * HALF, 2 * g : 2 * g + 2, :].rearrange("(t p) s k -> p t s k", p=P),
                )
                h_raw[(g, half)] = raw

        load_node_pair(0)
        w2_raw = weights.tile([P, PACK, WIDTH], BF16)
        nc.sync.dma_start(out=w2_raw[:], in_=ew2.rearrange("(p t) n -> p t n", t=PACK))
        for g in range(1, NODES // 2):
            load_node_pair(g)

        ident = consts.tile([P, P], F32)
        make_identity(nc, ident[:])

        w1_grouped = weights.tile([P, 2, CHUNKS, P, PACK], BF16, align_bytes=64)
        w1_codes = weights.tile([P, 2, WIDTH], U32, align_bytes=64)
        w1_scales = weights.tile([P, 2, WIDTH], U8, align_bytes=64)
        for a in range(2):
            nc.vector.tensor_copy(
                out=w1_grouped[:, a, :, :, :],
                in_=w1_raw[:, a, :, :].rearrange("q t (m c) -> q c m t", c=CHUNKS),
            )
        for a in range(2):
            nc.vector.quantize_mx(
                out=w1_codes[:, a, :].bitcast(FP8X4),
                scales=w1_scales[:, a, :],
                in_=w1_grouped[:, a, :, :, :].rearrange("q c m t -> q (c m t)"),
            )

        w2_grouped = weights.tile([P, WIDTH, PACK], BF16, align_bytes=64)
        w2_codes = weights.tile([P, WIDTH], U32, align_bytes=64)
        w2_scales = weights.tile([P, WIDTH], U8, align_bytes=64)

        def regroup(grouped, planes):
            nc.vector.tensor_copy(
                out=grouped[:].rearrange("p (c i) t -> p c t i", i=4),
                in_=planes[:].rearrange("p t (c i) -> p c t i", i=4),
            )

        h_codes = nodes.tile([P, NODES, CHAINS], U32, align_bytes=64)
        h_scales = nodes.tile([P, NODES, CHAINS], U8, align_bytes=64)
        h_grouped = {}

        def transpose_node(s, half):
            words = h_raw[(s // 2, half)][:].bitcast(F32)
            bank = aux_pool.tile([P, 2, HALF], F32, tag="aux")
            for u in range(2):
                for t in range(HALF_TILES):
                    first = (2 * t + s % 2) * WORDS + u * P
                    nc.tensor.transpose(bank[:, u, t * P : (t + 1) * P], words[:, first : first + P], ident[:])
            grouped = h_grouped_pool.tile([P, HALF * PACK], BF16, name="h_grouped", tag="h_grouped", align_bytes=64)
            nc.scalar.copy(
                out=grouped[:].bitcast(F32).rearrange("p (c u) -> p c u", u=2),
                in_=bank[:].rearrange("p u c -> p c u"),
            )
            h_grouped[(s, half)] = grouped

        def quantise_node(s, half):
            chains = slice(half * HALF, (half + 1) * HALF)
            nc.vector.quantize_mx(
                out=h_codes[:, s, chains].bitcast(FP8X4), scales=h_scales[:, s, chains], in_=h_grouped[(s, half)][:]
            )

        planes = {}
        hid_grouped = {}
        hid_codes = {}
        hid_scales = {}

        def layer1(i, half):
            chains = slice(half * HALF, (half + 1) * HALF)
            hidden = planes_pool.tile([P, CHUNKS, 2, HALF], BF16, name="planes", tag="planes")
            for c in range(CHUNKS):
                acc1 = acc1_pool.tile([P, 2, HALF], F32)
                for direction, joined in ((LR, (i, i + 1)), (RL, (i + 1, i))):
                    for a in range(2):
                        nc.tensor.matmul_mx(
                            out=acc1[:, direction, :],
                            lhsT=w1_codes[:, a, c * P : (c + 1) * P].bitcast(FP8X4),
                            lhsT_scale=w1_scales[:, a, c * P : (c + 1) * P],
                            rhs=h_codes[:, joined[a], chains].bitcast(FP8X4),
                            rhs_scale=h_scales[:, joined[a], chains],
                            start=(a == 0),
                            stop=(a == 1),
                        )
                nc.scalar.activation(
                    out=hidden[:, c, :, :], in_=acc1[:], func=RELU, bias=b1[:, c : c + 1], scale=1.0
                )
            planes[(i, half)] = hidden

        def regroup_hidden(i, half):
            grouped = hid_grouped_pool.tile([P, 2 * HALF, PACK], BF16, name="hid_grouped", tag="hid_grouped", align_bytes=64)
            regroup(grouped, planes[(i, half)][:].rearrange("p t d w -> p t (d w)"))
            hid_grouped[(i, half)] = grouped

        def quantise_hidden(i, half):
            codes = hid_pool.tile([P, 2 * HALF], U32, name="hid_codes", tag="hid_codes", align_bytes=64)
            scales = hid_pool.tile([P, 2 * HALF], U8, name="hid_scales", tag="hid_scales", align_bytes=64)
            nc.vector.quantize_mx(
                out=codes[:].bitcast(FP8X4),
                scales=scales[:],
                in_=hid_grouped[(i, half)][:].rearrange("p w t -> p (w t)"),
            )
            hid_codes[(i, half)] = codes
            hid_scales[(i, half)] = scales

        def layer2(j, half):
            messages = []
            if j > 0:
                messages.append((j - 1, LR))
            if j < EDGES:
                messages.append((j, RL))
            bias = b2_twice if len(messages) == 2 else b2_once
            for t in range(HALF_TILES):
                acc2 = aux_pool.tile([P, WIDTH], F32, tag="aux")
                for n, (i, direction) in enumerate(messages):
                    columns = slice(direction * HALF + t * P, direction * HALF + (t + 1) * P)
                    nc.tensor.matmul_mx(
                        out=acc2[:],
                        lhsT=hid_codes[(i, half)][:, columns].bitcast(FP8X4),
                        lhsT_scale=hid_scales[(i, half)][:, columns],
                        rhs=w2_codes[:].bitcast(FP8X4),
                        rhs_scale=w2_scales[:],
                        start=(n == 0),
                        stop=(n == len(messages) - 1),
                    )
                result = result_pool.tile([P, WIDTH], F32)
                nc.vector.tensor_tensor(out=result[:], in0=acc2[:], in1=bias[:], op=ADD)
                first_chain = half * HALF + t * P
                nc.sync.dma_start(out=out[first_chain : first_chain + P, j, :], in_=result[:])

        for half in range(HALVES):
            for s in range(2):
                transpose_node(s, half)
        for half in range(HALVES):
            for s in range(2):
                quantise_node(s, half)
        regroup(w2_grouped, w2_raw)

        def second_layer_after(unit):
            i, half = unit
            layer2(i, half)
            if i == EDGES - 1:
                layer2(NODES - 1, half)

        units = [(i, half) for i in range(EDGES) for half in range(HALVES)]
        for u, (i, half) in enumerate(units):
            layer1(i, half)
            if u == 0:
                spread_b2()
                nc.vector.quantize_mx(
                    out=w2_codes[:].bitcast(FP8X4),
                    scales=w2_scales[:],
                    in_=w2_grouped[:].rearrange("p w t -> p (w t)"),
                )
            if u >= LAG:
                second_layer_after(units[u - LAG])
            new_node = half == 0 and i + 2 < NODES
            if new_node:
                for other in range(HALVES):
                    transpose_node(i + 2, other)
            regroup_hidden(i, half)
            if new_node:
                for other in range(HALVES):
                    quantise_node(i + 2, other)
            quantise_hidden(i, half)
        for unit in units[len(units) - LAG :]:
            second_layer_after(unit)
